import numpy as np
import ml_dtypes


def mxq(x, axis, fmt="e4m3"):
    dtype, down = {"e4m3": (ml_dtypes.float8_e4m3fn, 7), "e5m2": (ml_dtypes.float8_e5m2, 14)}[fmt]
    v = np.moveaxis(np.asarray(x, np.float32).astype(ml_dtypes.bfloat16).astype(np.float64), axis, -1)
    blocks = v.reshape(v.shape[:-1] + (-1, 32))
    amax = np.abs(blocks).max(-1, keepdims=True)
    byte = np.maximum(np.where(amax > 0, np.frexp(amax)[1] - 1 + 127, 0) - down, 1)
    scale = np.exp2(byte - 127.0)
    codes = (blocks / scale).astype(np.float32).astype(dtype).astype(np.float64)
    return np.moveaxis((codes * scale).reshape(v.shape), -1, axis)


WIDE = False


def mx_kscale(k):
    if not WIDE:
        return np.ones(k)
    levels = np.array([18, -18])
    if k % 512:
        return np.exp2(np.random.permutation(np.resize(levels, k // 32))).repeat(32)
    a = np.empty((k // 512, 16))
    for p in range(k // 512):
        a[p, :8] = np.random.permutation(np.resize(levels, 8))
        for g in range(8):
            far = levels[np.abs(levels - a[p, g]) >= 10]
            a[p, g + 8] = far[np.random.randint(len(far))]
    return np.exp2(a.ravel()).repeat(32)


BF16 = ml_dtypes.bfloat16


def bf(x):
    return np.asarray(x, np.float32).astype(BF16)


def f64(x):
    return np.asarray(x).astype(np.float64)


B, S, D, H, DH = 4, 256, 2048, 8, 128
T, J = B * S, H * DH
ROPE_THETA = 10000.0


def rope_back(g, cos, sin):
    b, s, h, d = g.shape
    gr = g.reshape(b, s, h, d // 2, 2)
    g1, g2 = gr[..., 0], gr[..., 1]
    c = cos[None, :, None, :]
    sn = sin[None, :, None, :]
    d1 = g1 * c + g2 * sn
    d2 = g2 * c - g1 * sn
    return np.stack([d1, d2], axis=-1).reshape(b, s, h, d)


def setup_inputs():
    s = mx_kscale(T).reshape(B, S, 1)
    u = mx_kscale(J)
    inv_freq = 1.0 / ROPE_THETA ** (np.arange(0, DH, 2) / DH)
    ang = np.arange(S)[:, None] * inv_freq[None, :]
    x0 = bf(np.random.standard_normal((B, S, D)))
    w0 = bf(np.random.standard_normal((D, J)) / np.sqrt(D))
    g = np.random.standard_normal((B, S, H, DH)) * np.exp2(np.random.randint(-6, 1, (B, S, 1, 1))) * 2.0
    return {"x": bf(f64(x0) * s),
            "freqs_cos": bf(np.cos(ang)),
            "freqs_sin": bf(np.sin(ang)),
            "w_q": bf(f64(w0) / u),
            "grad_out": bf(g / s[..., None] * u.reshape(1, 1, H, DH))}


def reference(x, freqs_cos, freqs_sin, w_q, grad_out):
    dq = rope_back(f64(grad_out), f64(freqs_cos), f64(freqs_sin)).reshape(T, J)
    xf = f64(x).reshape(T, D)
    dx = (mxq(dq, 1, "e5m2") @ mxq(f64(w_q), 1, "e4m3").T).reshape(B, S, D)
    dw = mxq(xf, 0, "e4m3").T @ mxq(dq, 0, "e5m2")
    return dx, dw

@@ -1,0 +1,372 @@
+from contextlib import ExitStack
+
+import concourse.mybir as mybir
+from concourse.masks import make_identity
+
+F32 = mybir.dt.float32
+BF16 = mybir.dt.bfloat16
+U32 = mybir.dt.uint32
+U8 = mybir.dt.uint8
+E4 = mybir.dt.float8_e4m3fn_x4
+E5 = mybir.dt.float8_e5m2_x4
+MULT = mybir.AluOpType.mult
+ADD = mybir.AluOpType.add
+
+T, D, J = 1024, 2048, 1024
+P = 128
+FLOPS = 2 * 2 * T * D * J
+USE_G = True
+TAIL_HEADS = 1
+SLOTS = 14
+V_COLS = 128
+
+
+def tile_mla_pb_v_kernel(tc, x, freqs_cos, freqs_sin, w_q, grad_out, out_0, out_1):
+    nc = tc.nc
+    g_hbm = grad_out.rearrange("b s h d -> (b s) (h d)").rearrange("(g p j) f -> g p (j f)", g=2, j=4)
+    x_hbm = x.rearrange("b s d -> (b s) d").rearrange("(g p j) d -> g p j d", g=2, j=4)
+    w_hbm = w_q.rearrange("(a p t) f -> a p (t f)", p=P, t=2)
+    dx_hbm = out_0.rearrange("b s d -> (b s) d").rearrange("(g p j) d -> g j p d", g=2, j=4)
+    cos_hbm = freqs_cos.rearrange("(p j) i -> p (j i)", j=4)
+    sin_hbm = freqs_sin.rearrange("(p j) i -> p (j i)", j=4)
+
+    with ExitStack() as ctx:
+        keep = ctx.enter_context(tc.tile_pool(name="keep", bufs=1))
+        work = ctx.enter_context(tc.tile_pool(name="work", bufs=2))
+        psum = ctx.enter_context(tc.psum_pool(name="psum", bufs=7))
+        psum_tab = ctx.enter_context(tc.psum_pool(name="psum_tab", bufs=1))
+        ctx.enter_context(tc.manual_schedule())
+
+        trig = keep.tile([P, 2, 256], BF16, name="trig")
+        for k, src in enumerate((cos_hbm, sin_hbm)):
+            for half in range(2):
+                nc.scalar.dma_start(out=trig[64 * half : 64 * half + 64, k, :], in_=src)
+
+        g_sb = {}
+        w_sb = {}
+        x_sb = {}
+
+        def load_g(g, j0, j1):
+            tile = keep.tile([P, (j1 - j0) * J], BF16, name="g%d_%d" % (g, j0))
+            nc.sync.dma_start(out=tile[:], in_=g_hbm[g][:, j0 * J : j1 * J])
+            for j in range(j0, j1):
+                g_sb[4 * g + j] = tile[:, (j - j0) * J : (j - j0 + 1) * J]
+
+        def load_w(a):
+            tile = work.tile([P, 2 * J], BF16, name="w%d" % a, tag="slot", bufs=SLOTS)
+            nc.sync.dma_start(out=tile[:], in_=w_hbm[a])
+            w_sb[a] = tile
+
+        def load_x(g, h):
+            tile = keep.tile([P, 4, 1024], BF16, name="x%d_%d" % (g, h))
+            nc.sync.dma_start(out=tile[:], in_=x_hbm[g][:, :, 1024 * h : 1024 * (h + 1)])
+            x_sb[g, h] = tile
+
+        load_g(0, 0, 1)
+        load_w(0)
+        load_g(0, 1, 2)
+        load_w(1)
+        load_g(0, 2, 4)
+        for a in range(2, 8):
+            load_w(a)
+        load_g(1, 0, 4)
+        for h in range(2):
+            for g in range(2):
+                load_x(g, h)
+
+        ident = keep.tile([P, P], F32, name="ident")
+        make_identity(nc, ident[:])
+
+        sign = keep.tile([P, 2], F32, name="sign")
+        nc.vector.memset(sign[:, 0:1], 1.0)
+        nc.vector.memset(sign[:, 1:2], -1.0)
+        tab = keep.tile([P, 1024], BF16, name="tab")
+        shape = [P, 2, 128, 2]
+        cos_in = trig[:, 0, :].rearrange("p (a u) -> p u a", u=2).unsqueeze(3).broadcast_to(shape)
+        sin_in = trig[:, 1, :].rearrange("p (a u) -> p u a", u=2).unsqueeze(3).broadcast_to(shape)
+        nc.scalar.copy(out=tab[:, 0:512].rearrange("p (u a e) -> p u a e", u=2, e=2), in_=cos_in)
+        nc.vector.tensor_tensor(
+            out=tab[:, 512:1024].rearrange("p (u a e) -> p u a e", u=2, e=2),
+            in0=sin_in,
+            in1=sign[:].unsqueeze(1).unsqueeze(1).broadcast_to(shape),
+            op=MULT,
+        )
+
+        def new_bank():
+            bank = psum.tile([P, 512], F32, name="bank")
+            return bank
+
+        tab_ps = psum_tab.tile([P, 512], F32, name="tab_ps")
+        tab_t = keep.tile([P, 512], F32, name="tab_t")
+
+        def table_there():
+            bank = new_bank()
+            words = tab[:].bitcast(F32)
+            for k in range(4):
+                nc.tensor.transpose(bank[:, k * P : (k + 1) * P], words[:, k * P : (k + 1) * P], ident[:])
+            nc.scalar.copy(out=tab_t[:], in_=bank[:])
+
+        def table_back():
+            for k in range(4):
+                nc.tensor.transpose(tab_ps[:, k * P : (k + 1) * P], tab_t[:, k * P : (k + 1) * P], ident[:])
+
+        def codes(name, width):
+            c = keep.tile([P, width], U32, name=name + "c", align_bytes=64)
+            s = keep.tile([P, width], U8, name=name + "s", align_bytes=64)
+            return c, s
+
+        w_mx = {(c, q): codes("w%d_%d" % (c, q), 512) for c in range(4) for q in range(2)}
+        dqt_mx = {s: codes("dqt%d" % s, 256) for s in range(8)}
+        dqk_mx = {(g, q): codes("dqk%d_%d" % (g, q), 512) for g in range(2) for q in range(2)}
+        dq = {}
+        for g in range(2):
+            dq[g] = keep.tile([P, 4 * J], BF16, name="dq%d" % g, align_bytes=64)
+        prod = {}
+        w_t = {}
+        dq_t = {}
+        dq_k = {}
+        x_k = {}
+        x_mx = {}
+        stage = {}
+
+        def table(s, k, h0, h1):
+            src = tab[:] if (s == 0 or not USE_G) else tab_ps[:].bitcast(BF16)
+            rows = src[:, 512 * k : 512 * (k + 1)].rearrange("p (u j w e) -> p u j w e", u=2, j=4, e=2)
+            return rows[:, :, s % 4, :, :].unsqueeze(2).broadcast_to([P, 2, h1 - h0, 32, 2])
+
+        def mul(s, k, h0=0, h1=8):
+            if (s, k) not in prod:
+                prod[s, k] = work.tile([P, J], F32, name="prod%d" % k)
+            gv = g_sb[s].rearrange("p (h w u e) -> p u h w e", h=8, u=2, e=2)[:, :, h0:h1]
+            if k == 1:
+                gv = gv[:, :, :, :, ::-1]
+            out = prod[s, k][:].rearrange("p (u h w e) -> p u h w e", u=2, h=8, e=2)[:, :, h0:h1]
+            nc.vector.tensor_tensor(out=out, in0=gv, in1=table(s, k, h0, h1), op=MULT)
+
+        def add(s, eng, lo, hi):
+            out = dq[s // 4][:, (s % 4) * J + lo : (s % 4) * J + hi]
+            eng.tensor_tensor(out=out, in0=prod[s, 0][:, lo:hi], in1=prod[s, 1][:, lo:hi], op=ADD)
+
+        def quantize(pair, src, fmt):
+            nc.vector.quantize_mx(out=pair[0][:].bitcast(fmt), scales=pair[1][:], in_=src)
+
+        def turn_w(a, q):
+            c = a // 2
+            if (c, q) not in w_t:
+                w_t[c, q] = work.tile([P, 1024], F32, name="w_t", bufs=4, align_bytes=64)
+            bank = new_bank()
+            words = w_sb[a][:].bitcast(F32)
+            for t in range(2):
+                for u in range(2):
+                    lo = t * 512 + q * 256
+                    k = 2 * t + u
+                    nc.tensor.transpose(bank[:, k * P : (k + 1) * P], words[:, lo + u : lo + 256 : 2], ident[:])
+            out = w_t[c, q][:, 512 * (a % 2) : 512 * (a % 2 + 1)].rearrange("p (r k) -> p r k", k=4)
+            nc.scalar.copy(out=out, in_=bank[:].rearrange("p (k r) -> p r k", k=4))
+
+        def turn_w_chunk(c):
+            for a in (2 * c, 2 * c + 1):
+                for q in range(2):
+                    turn_w(a, q)
+
+        def quant_w(c):
+            for q in range(2):
+                quantize(w_mx[c, q], w_t[c, q][:].bitcast(BF16), E4)
+
+        def turn_dq(s):
+            bank = new_bank()
+            words = dq[s // 4][:, (s % 4) * J : (s % 4 + 1) * J].bitcast(F32)
+            for q in range(2):
+                for u in range(2):
+                    lo = u * 256 + q * P
+                    k = 2 * q + u
+                    nc.tensor.transpose(bank[:, k * P : (k + 1) * P], words[:, lo : lo + P], ident[:])
+            dq_t[s] = work.tile([P, 512], F32, name="dq_t", align_bytes=64)
+            nc.scalar.copy(
+                out=dq_t[s][:].rearrange("p (q r u) -> p q r u", q=2, u=2),
+                in_=bank[:].rearrange("p (q u r) -> p q r u", q=2, u=2),
+            )
+
+        def quant_dq(s):
+            quantize(dqt_mx[s], dq_t[s][:].bitcast(BF16), E5)
+
+        def weave_dq(g, q):
+            dq_k[g, q] = work.tile([P, 2048], BF16, name="woven", bufs=4, align_bytes=64)
+            src = dq[g][:].rearrange("p (j u q c i) -> p q u c j i", j=4, u=2, q=2, i=4)[:, q]
+            nc.vector.tensor_copy(out=dq_k[g, q][:].rearrange("p (u c i j) -> p u c j i", u=2, i=4, j=4), in_=src)
+
+        def quant_dqk(g, q):
+            quantize(dqk_mx[g, q], dq_k[g, q][:], E5)
+
+        def weave_x(m0, n, g):
+            x_k[m0, g] = work.tile([P, 512 * n], BF16, name="woven", bufs=4, align_bytes=64)
+            lo = (m0 % 8) * P
+            src = x_sb[g, m0 // 8][:, :, lo : lo + n * P].rearrange("p j (c i) -> p c j i", i=4)
+            dst = x_k[m0, g][:].rearrange("p (c i j) -> p c j i", i=4, j=4)
+            nc.vector.tensor_copy(out=dst, in_=src)
+
+        def quant_x(m0, n, g):
+            xc = work.tile([P, n * P], U32, name="xc", bufs=6, align_bytes=64)
+            xs = work.tile([P, n * P], U8, name="xs", bufs=6, align_bytes=64)
+            quantize((xc, xs), x_k[m0, g][:], E4)
+            for k in range(n):
+                x_mx[m0 + k, g] = (xc[:, k * P : (k + 1) * P], xs[:, k * P : (k + 1) * P])
+
+        def product(lhs, cols, lhs_fmt, rhs, rhs_fmt):
+            bank = new_bank()
+            for k in range(2):
+                nc.tensor.matmul_mx(
+                    out=bank[:],
+                    lhsT=lhs[k][0][:, cols[k]].bitcast(lhs_fmt),
+                    lhsT_scale=lhs[k][1][:, cols[k]],
+                    rhs=rhs[k][0][:].bitcast(rhs_fmt),
+                    rhs_scale=rhs[k][1][:],
+                    start=(k == 0),
+                    stop=(k == 1),
+                )
+            return bank
+
+        def evac(out, in_, on_vector):
+            if on_vector:
+                nc.vector.tensor_copy(out=out, in_=in_)
+            else:
+                nc.scalar.copy(out=out, in_=in_)
+
+        def dx_bank(s, c, on_vector=False):
+            bank = product([dqt_mx[s]] * 2, [slice(0, P), slice(P, 2 * P)], E5, [w_mx[c, 0], w_mx[c, 1]], E4)
+            key = ("dx", s, c // 2)
+            if key not in stage:
+                stage[key] = work.tile([P, 1024], F32, name="stage", tag="slot", bufs=SLOTS)
+            evac(stage[key][:, 512 * (c % 2) : 512 * (c % 2 + 1)], bank[:], on_vector)
+            if c % 2 == 1:
+                h = c // 2
+                nc.sync.dma_start(out=dx_hbm[s // 4][s % 4][:, 1024 * h : 1024 * (h + 1)], in_=stage[key][:])
+
+        def dw_bank(m, q, on_vector=False, split=False):
+            cols = slice(0, P)
+            bank = product([x_mx[m, 0], x_mx[m, 1]], [cols, cols], E4, [dqk_mx[0, q], dqk_mx[1, q]], E5)
+            key = ("dw", m)
+            if key not in stage:
+                stage[key] = work.tile([P, 1024], F32, name="stage", tag="slot", bufs=SLOTS)
+            half = stage[key][:, 512 * q : 512 * (q + 1)]
+            evac(half.rearrange("p (w u e) -> p w u e", u=2, e=2), bank[:].rearrange("p (u w e) -> p w u e", u=2, e=2), on_vector)
+            if split:
+                nc.sync.dma_start(out=out_1[m * P : (m + 1) * P, 512 * q : 512 * (q + 1)], in_=half)
+            elif q == 1:
+                nc.sync.dma_start(out=out_1[m * P : (m + 1) * P, :], in_=stage[key][:])
+
+        def rotate_head(s):
+            mul(s, 0)
+            if USE_G and s < 7:
+                mul(s, 1, 0, 8 - TAIL_HEADS)
+            else:
+                mul(s, 1)
+
+        def rotate_tail(s):
+            if USE_G and s < 7:
+                if V_COLS:
+                    add(s, nc.vector, 0, V_COLS)
+                mul(s, 1, 8 - TAIL_HEADS, 8)
+                add(s, nc.gpsimd, V_COLS, J)
+            else:
+                add(s, nc.vector, 0, J)
+
+        table_there()
+        turn_w(0, 0)
+        turn_w(0, 1)
+        table_back()
+        turn_w(1, 0)
+        turn_w(1, 1)
+        rotate_head(0)
+        rotate_tail(0)
+        rotate_head(1)
+        quant_w(0)
+        rotate_tail(1)
+        turn_w_chunk(1)
+        turn_dq(0)
+        rotate_head(2)
+        quant_dq(0)
+        quant_w(1)
+        rotate_tail(2)
+        turn_w_chunk(2)
+        turn_dq(1)
+        dx_bank(0, 0)
+        dx_bank(0, 1)
+        rotate_head(3)
+        quant_dq(1)
+        quant_w(2)
+        rotate_tail(3)
+        turn_w(6, 0)
+        turn_w(6, 1)
+        dx_bank(1, 0)
+        turn_w(7, 0)
+        turn_w(7, 1)
+        turn_dq(2)
+        dx_bank(1, 1)
+        rotate_head(4)
+        quant_w(3)
+        quant_dq(2)
+        rotate_tail(4)
+        dx_bank(0, 2)
+        dx_bank(1, 2)
+        turn_dq(3)
+        dx_bank(2, 0)
+        dx_bank(2, 1)
+        dx_bank(0, 3)
+        dx_bank(1, 3)
+        rotate_head(5)
+        quant_dq(3)
+        rotate_tail(5)
+        turn_dq(4)
+        dx_bank(2, 2)
+        dx_bank(2, 3)
+        rotate_head(6)
+        quant_dq(4)
+        rotate_tail(6)
+        for c in range(2):
+            dx_bank(3, c)
+        turn_dq(5)
+        for c in range(2, 4):
+            dx_bank(3, c)
+        rotate_head(7)
+        quant_dq(5)
+        rotate_tail(7)
+        turn_dq(6)
+        for c in range(4):
+            dx_bank(4, c)
+        turn_dq(7)
+        weave_dq(0, 0)
+        quant_dq(6)
+        weave_dq(1, 0)
+        quant_dq(7)
+        quant_dqk(0, 0)
+        weave_x(0, 2, 0)
+        quant_dqk(1, 0)
+        weave_x(0, 2, 1)
+        quant_x(0, 2, 0)
+        weave_dq(0, 1)
+        quant_x(0, 2, 1)
+        weave_dq(1, 1)
+        quant_dqk(0, 1)
+        weave_x(2, 2, 0)
+        quant_dqk(1, 1)
+        for s in range(5, 8):
+            for c in range(4):
+                dx_bank(s, c)
+        for q in range(2):
+            for m in range(2):
+                dw_bank(m, q, split=True)
+        pieces = [(m0, 2) for m0 in range(2, 16, 2)]
+        weave_x(2, 2, 1)
+        quant_x(2, 2, 0)
+        for k, (m0, n) in enumerate(pieces):
+            nxt = pieces[k + 1] if k + 1 < len(pieces) else None
+            if nxt:
+                weave_x(nxt[0], nxt[1], 0)
+            quant_x(m0, n, 1)
+            if nxt:
+                weave_x(nxt[0], nxt[1], 1)
+                quant_x(nxt[0], nxt[1], 0)
+            for m in range(m0, m0 + n):
+                for q in range(2):
+                    dw_bank(m, q, on_vector=(m >= 14 and q == 1), split=(m == 15))

@@ -17,14 +17,16 @@ P = 128
 FLOPS = 2 * 2 * T * D * J
 USE_G = True
 TAIL_HEADS = 1
-SLOTS = 14
-V_COLS = 128
+SLOTS = 13
+V_COLS = 256
+A_WEAVES = 1
+V_FROM = 5
 
 
 def tile_mla_pb_v_kernel(tc, x, freqs_cos, freqs_sin, w_q, grad_out, out_0, out_1):
     nc = tc.nc
     g_hbm = grad_out.rearrange("b s h d -> (b s) (h d)").rearrange("(g p j) f -> g p (j f)", g=2, j=4)
-    x_hbm = x.rearrange("b s d -> (b s) d").rearrange("(g p j) d -> g p j d", g=2, j=4)
+    x_hbm = x.rearrange("b s d -> (b s) d").rearrange("(g p j) d -> g p (j d)", g=2, j=4)
     w_hbm = w_q.rearrange("(a p t) f -> a p (t f)", p=P, t=2)
     dx_hbm = out_0.rearrange("b s d -> (b s) d").rearrange("(g p j) d -> g j p d", g=2, j=4)
     cos_hbm = freqs_cos.rearrange("(p j) i -> p (j i)", j=4)
@@ -40,11 +42,11 @@ def tile_mla_pb_v_kernel(tc, x, freqs_cos, freqs_sin, w_q, grad_out, out_0, out_
         trig = keep.tile([P, 2, 256], BF16, name="trig")
         for k, src in enumerate((cos_hbm, sin_hbm)):
             for half in range(2):
-                nc.scalar.dma_start(out=trig[64 * half : 64 * half + 64, k, :], in_=src)
+                nc.sync.dma_start(out=trig[64 * half : 64 * half + 64, k, :], in_=src)
 
         g_sb = {}
         w_sb = {}
-        x_sb = {}
+        x_sb = keep.tile([P, 2 * 4 * D], BF16, name="x_sb")
 
         def load_g(g, j0, j1):
             tile = keep.tile([P, (j1 - j0) * J], BF16, name="g%d_%d" % (g, j0))
@@ -57,22 +59,17 @@ def tile_mla_pb_v_kernel(tc, x, freqs_cos, freqs_sin, w_q, grad_out, out_0, out_
             nc.sync.dma_start(out=tile[:], in_=w_hbm[a])
             w_sb[a] = tile
 
-        def load_x(g, h):
-            tile = keep.tile([P, 4, 1024], BF16, name="x%d_%d" % (g, h))
-            nc.sync.dma_start(out=tile[:], in_=x_hbm[g][:, :, 1024 * h : 1024 * (h + 1)])
-            x_sb[g, h] = tile
-
         load_g(0, 0, 1)
         load_w(0)
         load_g(0, 1, 2)
         load_w(1)
+        load_w(2)
         load_g(0, 2, 4)
-        for a in range(2, 8):
+        for a in range(3, 8):
             load_w(a)
         load_g(1, 0, 4)
-        for h in range(2):
-            for g in range(2):
-                load_x(g, h)
+        for g in range(2):
+            nc.sync.dma_start(out=x_sb[:, g * 4 * D : (g + 1) * 4 * D], in_=x_hbm[g])
 
         ident = keep.tile([P, P], F32, name="ident")
         make_identity(nc, ident[:])
@@ -115,12 +112,15 @@ def tile_mla_pb_v_kernel(tc, x, freqs_cos, freqs_sin, w_q, grad_out, out_0, out_
             s = keep.tile([P, width], U8, name=name + "s", align_bytes=64)
             return c, s
 
-        w_mx = {(c, q): codes("w%d_%d" % (c, q), 512) for c in range(4) for q in range(2)}
+        w_mx = {c: codes("w%d" % c, 1024) for c in range(4)}
         dqt_mx = {s: codes("dqt%d" % s, 256) for s in range(8)}
-        dqk_mx = {(g, q): codes("dqk%d_%d" % (g, q), 512) for g in range(2) for q in range(2)}
-        dq = {}
-        for g in range(2):
-            dq[g] = keep.tile([P, 4 * J], BF16, name="dq%d" % g, align_bytes=64)
+        dqk_mx = {q: codes("dqk%d" % q, 1024) for q in range(2)}
+        dq = keep.tile([P, 8 * J], BF16, name="dq", align_bytes=64)
+
+        def dq_slab(s):
+            lo = (2 * (s % 4) + s // 4) * J
+            return dq[:, lo : lo + J]
+
         prod = {}
         w_t = {}
         dq_t = {}
@@ -144,7 +144,7 @@ def tile_mla_pb_v_kernel(tc, x, freqs_cos, freqs_sin, w_q, grad_out, out_0, out_
             nc.vector.tensor_tensor(out=out, in0=gv, in1=table(s, k, h0, h1), op=MULT)
 
         def add(s, eng, lo, hi):
-            out = dq[s // 4][:, (s % 4) * J + lo : (s % 4) * J + hi]
+            out = dq_slab(s)[:, lo:hi]
             eng.tensor_tensor(out=out, in0=prod[s, 0][:, lo:hi], in1=prod[s, 1][:, lo:hi], op=ADD)
 
         def quantize(pair, src, fmt):
@@ -152,8 +152,8 @@ def tile_mla_pb_v_kernel(tc, x, freqs_cos, freqs_sin, w_q, grad_out, out_0, out_
 
         def turn_w(a, q):
             c = a // 2
-            if (c, q) not in w_t:
-                w_t[c, q] = work.tile([P, 1024], F32, name="w_t", bufs=4, align_bytes=64)
+            if c not in w_t:
+                w_t[c] = work.tile([P, 2048], F32, name="w_t", tag="wide", align_bytes=64)
             bank = new_bank()
             words = w_sb[a][:].bitcast(F32)
             for t in range(2):
@@ -161,7 +161,8 @@ def tile_mla_pb_v_kernel(tc, x, freqs_cos, freqs_sin, w_q, grad_out, out_0, out_
                     lo = t * 512 + q * 256
                     k = 2 * t + u
                     nc.tensor.transpose(bank[:, k * P : (k + 1) * P], words[:, lo + u : lo + 256 : 2], ident[:])
-            out = w_t[c, q][:, 512 * (a % 2) : 512 * (a % 2 + 1)].rearrange("p (r k) -> p r k", k=4)
+            lo = 1024 * q + 512 * (a % 2)
+            out = w_t[c][:, lo : lo + 512].rearrange("p (r k) -> p r k", k=4)
             nc.scalar.copy(out=out, in_=bank[:].rearrange("p (k r) -> p r k", k=4))
 
         def turn_w_chunk(c):
@@ -170,12 +171,11 @@ def tile_mla_pb_v_kernel(tc, x, freqs_cos, freqs_sin, w_q, grad_out, out_0, out_
                     turn_w(a, q)
 
         def quant_w(c):
-            for q in range(2):
-                quantize(w_mx[c, q], w_t[c, q][:].bitcast(BF16), E4)
+            quantize(w_mx[c], w_t[c][:].bitcast(BF16), E4)
 
         def turn_dq(s):
             bank = new_bank()
-            words = dq[s // 4][:, (s % 4) * J : (s % 4 + 1) * J].bitcast(F32)
+            words = dq_slab(s).bitcast(F32)
             for q in range(2):
                 for u in range(2):
                     lo = u * 256 + q * P
@@ -190,37 +190,40 @@ def tile_mla_pb_v_kernel(tc, x, freqs_cos, freqs_sin, w_q, grad_out, out_0, out_
         def quant_dq(s):
             quantize(dqt_mx[s], dq_t[s][:].bitcast(BF16), E5)
 
-        def weave_dq(g, q):
-            dq_k[g, q] = work.tile([P, 2048], BF16, name="woven", bufs=4, align_bytes=64)
-            src = dq[g][:].rearrange("p (j u q c i) -> p q u c j i", j=4, u=2, q=2, i=4)[:, q]
-            nc.vector.tensor_copy(out=dq_k[g, q][:].rearrange("p (u c i j) -> p u c j i", u=2, i=4, j=4), in_=src)
+        def weave_dq(q):
+            dq_k[q] = work.tile([P, 4096], BF16, name="dq_k", tag="wide", align_bytes=64)
+            src = dq[:].rearrange("p (j n q c i) -> p q n c j i", j=4, n=4, q=2, i=4)[:, q]
+            nc.vector.tensor_copy(out=dq_k[q][:].rearrange("p (n c i j) -> p n c j i", n=4, i=4, j=4), in_=src)
 
-        def quant_dqk(g, q):
-            quantize(dqk_mx[g, q], dq_k[g, q][:], E5)
+        def quant_dqk(q):
+            quantize(dqk_mx[q], dq_k[q][:], E5)
 
-        def weave_x(m0, n, g):
-            x_k[m0, g] = work.tile([P, 512 * n], BF16, name="woven", bufs=4, align_bytes=64)
-            lo = (m0 % 8) * P
-            src = x_sb[g, m0 // 8][:, :, lo : lo + n * P].rearrange("p j (c i) -> p c j i", i=4)
-            dst = x_k[m0, g][:].rearrange("p (c i j) -> p c j i", i=4, j=4)
-            nc.vector.tensor_copy(out=dst, in_=src)
+        def weave_x(k, on_scalar=False):
+            x_k[k] = work.tile([P, 2048], BF16, name="x_k", bufs=3, align_bytes=64)
+            src = x_sb[:].rearrange("p (g j k c i) -> p k g c j i", g=2, j=4, k=8, i=4)[:, k]
+            dst = x_k[k][:].rearrange("p (g c i j) -> p g c j i", g=2, i=4, j=4)
+            if on_scalar:
+                nc.scalar.copy(out=dst, in_=src)
+            else:
+                nc.vector.tensor_copy(out=dst, in_=src)
 
-        def quant_x(m0, n, g):
-            xc = work.tile([P, n * P], U32, name="xc", bufs=6, align_bytes=64)
-            xs = work.tile([P, n * P], U8, name="xs", bufs=6, align_bytes=64)
-            quantize((xc, xs), x_k[m0, g][:], E4)
-            for k in range(n):
-                x_mx[m0 + k, g] = (xc[:, k * P : (k + 1) * P], xs[:, k * P : (k + 1) * P])
+        def quant_x(k):
+            xc = work.tile([P, 512], U32, name="xc", bufs=7, align_bytes=64)
+            xs = work.tile([P, 512], U8, name="xs", bufs=7, align_bytes=64)
+            x_mx[k] = (xc, xs)
+            quantize(x_mx[k], x_k[k][:], E4)
 
-        def product(lhs, cols, lhs_fmt, rhs, rhs_fmt):
+        def product(lhs, lhs_lo, lhs_step, lhs_fmt, rhs, rhs_fmt):
             bank = new_bank()
             for k in range(2):
+                m_cols = slice(lhs_lo + k * lhs_step, lhs_lo + k * lhs_step + P)
+                n_cols = slice(512 * k, 512 * (k + 1))
                 nc.tensor.matmul_mx(
                     out=bank[:],
-                    lhsT=lhs[k][0][:, cols[k]].bitcast(lhs_fmt),
-                    lhsT_scale=lhs[k][1][:, cols[k]],
-                    rhs=rhs[k][0][:].bitcast(rhs_fmt),
-                    rhs_scale=rhs[k][1][:],
+                    lhsT=lhs[0][:, m_cols].bitcast(lhs_fmt),
+                    lhsT_scale=lhs[1][:, m_cols],
+                    rhs=rhs[0][:, n_cols].bitcast(rhs_fmt),
+                    rhs_scale=rhs[1][:, n_cols],
                     start=(k == 0),
                     stop=(k == 1),
                 )
@@ -233,7 +236,7 @@ def tile_mla_pb_v_kernel(tc, x, freqs_cos, freqs_sin, w_q, grad_out, out_0, out_
                 nc.scalar.copy(out=out, in_=in_)
 
         def dx_bank(s, c, on_vector=False):
-            bank = product([dqt_mx[s]] * 2, [slice(0, P), slice(P, 2 * P)], E5, [w_mx[c, 0], w_mx[c, 1]], E4)
+            bank = product(dqt_mx[s], 0, P, E5, w_mx[c], E4)
             key = ("dx", s, c // 2)
             if key not in stage:
                 stage[key] = work.tile([P, 1024], F32, name="stage", tag="slot", bufs=SLOTS)
@@ -243,8 +246,7 @@ def tile_mla_pb_v_kernel(tc, x, freqs_cos, freqs_sin, w_q, grad_out, out_0, out_
                 nc.sync.dma_start(out=dx_hbm[s // 4][s % 4][:, 1024 * h : 1024 * (h + 1)], in_=stage[key][:])
 
         def dw_bank(m, q, on_vector=False, split=False):
-            cols = slice(0, P)
-            bank = product([x_mx[m, 0], x_mx[m, 1]], [cols, cols], E4, [dqk_mx[0, q], dqk_mx[1, q]], E5)
+            bank = product(x_mx[m // 2], (m % 2) * P, 256, E4, dqk_mx[q], E5)
             key = ("dw", m)
             if key not in stage:
                 stage[key] = work.tile([P, 1024], F32, name="stage", tag="slot", bufs=SLOTS)
@@ -282,91 +284,80 @@ def tile_mla_pb_v_kernel(tc, x, freqs_cos, freqs_sin, w_q, grad_out, out_0, out_
         rotate_head(1)
         quant_w(0)
         rotate_tail(1)
-        turn_w_chunk(1)
+        turn_w(2, 0)
+        turn_w(2, 1)
         turn_dq(0)
+        turn_w(3, 0)
+        turn_w(3, 1)
         rotate_head(2)
         quant_dq(0)
         quant_w(1)
         rotate_tail(2)
-        turn_w_chunk(2)
+        turn_w(4, 0)
+        turn_w(4, 1)
         turn_dq(1)
+        turn_w(5, 0)
+        turn_w(5, 1)
         dx_bank(0, 0)
+        turn_w(6, 0)
+        turn_w(6, 1)
         dx_bank(0, 1)
         rotate_head(3)
         quant_dq(1)
         quant_w(2)
         rotate_tail(3)
-        turn_w(6, 0)
-        turn_w(6, 1)
-        dx_bank(1, 0)
         turn_w(7, 0)
         turn_w(7, 1)
         turn_dq(2)
+        dx_bank(1, 0)
         dx_bank(1, 1)
+        dx_bank(0, 2)
+        dx_bank(1, 2)
         rotate_head(4)
         quant_w(3)
         quant_dq(2)
         rotate_tail(4)
-        dx_bank(0, 2)
-        dx_bank(1, 2)
         turn_dq(3)
-        dx_bank(2, 0)
-        dx_bank(2, 1)
         dx_bank(0, 3)
         dx_bank(1, 3)
-        rotate_head(5)
-        quant_dq(3)
-        rotate_tail(5)
-        turn_dq(4)
-        dx_bank(2, 2)
-        dx_bank(2, 3)
-        rotate_head(6)
-        quant_dq(4)
-        rotate_tail(6)
-        for c in range(2):
-            dx_bank(3, c)
-        turn_dq(5)
-        for c in range(2, 4):
-            dx_bank(3, c)
-        rotate_head(7)
-        quant_dq(5)
-        rotate_tail(7)
-        turn_dq(6)
-        for c in range(4):
-            dx_bank(4, c)
-        turn_dq(7)
-        weave_dq(0, 0)
-        quant_dq(6)
-        weave_dq(1, 0)
-        quant_dq(7)
-        quant_dqk(0, 0)
-        weave_x(0, 2, 0)
-        quant_dqk(1, 0)
-        weave_x(0, 2, 1)
-        quant_x(0, 2, 0)
-        weave_dq(0, 1)
-        quant_x(0, 2, 1)
-        weave_dq(1, 1)
-        quant_dqk(0, 1)
-        weave_x(2, 2, 0)
-        quant_dqk(1, 1)
         for s in range(5, 8):
-            for c in range(4):
-                dx_bank(s, c)
+            rotate_head(s)
+            quant_dq(s - 2)
+            rotate_tail(s)
+            for c in range(2):
+                dx_bank(s - 3, c)
+            turn_dq(s - 1)
+            for c in range(2, 4):
+                dx_bank(s - 3, c)
+        quant_dq(6)
+        turn_dq(7)
+        weave_x(0, on_scalar=True)
+        for c in range(2):
+            dx_bank(5, c)
+        for c in range(2, 4):
+            dx_bank(5, c)
+        weave_dq(0)
+        quant_dq(7)
+        quant_dqk(0)
+        quant_x(0)
+        weave_dq(1)
+        for c in range(4):
+            dx_bank(6, c)
+        weave_x(1)
+        quant_dqk(1)
+        for c in range(4):
+            dx_bank(7, c)
         for q in range(2):
             for m in range(2):
                 dw_bank(m, q, split=True)
-        pieces = [(m0, 2) for m0 in range(2, 16, 2)]
-        weave_x(2, 2, 1)
-        quant_x(2, 2, 0)
-        for k, (m0, n) in enumerate(pieces):
-            nxt = pieces[k + 1] if k + 1 < len(pieces) else None
-            if nxt:
-                weave_x(nxt[0], nxt[1], 0)
-            quant_x(m0, n, 1)
-            if nxt:
-                weave_x(nxt[0], nxt[1], 1)
-                quant_x(nxt[0], nxt[1], 0)
-            for m in range(m0, m0 + n):
-                for q in range(2):
-                    dw_bank(m, q, on_vector=(m >= 14 and q == 1), split=(m == 15))
+        for k in range(1, 8):
+            if k < 7:
+                weave_x(k + 1)
+            quant_x(k)
+            if k == 6:
+                for m in (2, 3):
+                    for q in range(2):
+                        dw_bank(m, q)
+        for m in range(4, 16):
+            for q in range(2):
+                dw_bank(m, q, on_vector=(m >= 2 * V_FROM and q == 1), split=(m == 15))

@@ -7,57 +7,57 @@ F32 = mybir.dt.float32
 BF16 = mybir.dt.bfloat16
 U32 = mybir.dt.uint32
 U8 = mybir.dt.uint8
-E4 = mybir.dt.float8_e4m3fn_x4
-E5 = mybir.dt.float8_e5m2_x4
+E4M3 = mybir.dt.float8_e4m3fn_x4
+E5M2 = mybir.dt.float8_e5m2_x4
 MULT = mybir.AluOpType.mult
 ADD = mybir.AluOpType.add
 
 T, D, J = 1024, 2048, 1024
-P = 128
 FLOPS = 2 * 2 * T * D * J
-USE_G = True
-TAIL_HEADS = 1
-SLOTS = 13
-V_COLS = 256
-A_WEAVES = 1
-V_FROM = 5
+P = 128
+BANK = 512
+HEADS = 8
+SLABS = 8
+W_TILES = 8
+X_PIECES = 8
+
+VECTOR_SUMS = 256
+SHARED_FROM = 5
+ROW_BUFFERS = W_TILES + 5
 
 
 def tile_mla_pb_v_kernel(tc, x, freqs_cos, freqs_sin, w_q, grad_out, out_0, out_1):
     nc = tc.nc
     g_hbm = grad_out.rearrange("b s h d -> (b s) (h d)").rearrange("(g p j) f -> g p (j f)", g=2, j=4)
     x_hbm = x.rearrange("b s d -> (b s) d").rearrange("(g p j) d -> g p (j d)", g=2, j=4)
-    w_hbm = w_q.rearrange("(a p t) f -> a p (t f)", p=P, t=2)
     dx_hbm = out_0.rearrange("b s d -> (b s) d").rearrange("(g p j) d -> g j p d", g=2, j=4)
-    cos_hbm = freqs_cos.rearrange("(p j) i -> p (j i)", j=4)
-    sin_hbm = freqs_sin.rearrange("(p j) i -> p (j i)", j=4)
+    w_hbm = w_q.rearrange("(a p t) f -> a p (t f)", p=P, t=2)
 
     with ExitStack() as ctx:
         keep = ctx.enter_context(tc.tile_pool(name="keep", bufs=1))
         work = ctx.enter_context(tc.tile_pool(name="work", bufs=2))
         psum = ctx.enter_context(tc.psum_pool(name="psum", bufs=7))
-        psum_tab = ctx.enter_context(tc.psum_pool(name="psum_tab", bufs=1))
+        psum_table = ctx.enter_context(tc.psum_pool(name="psum_table", bufs=1))
         ctx.enter_context(tc.manual_schedule())
 
         trig = keep.tile([P, 2, 256], BF16, name="trig")
-        for k, src in enumerate((cos_hbm, sin_hbm)):
+        for k, src in enumerate((freqs_cos, freqs_sin)):
             for half in range(2):
-                nc.sync.dma_start(out=trig[64 * half : 64 * half + 64, k, :], in_=src)
+                rows = src.rearrange("(p j) i -> p (j i)", j=4)
+                nc.sync.dma_start(out=trig[64 * half : 64 * half + 64, k, :], in_=rows)
 
-        g_sb = {}
-        w_sb = {}
-        x_sb = keep.tile([P, 2 * 4 * D], BF16, name="x_sb")
+        g_slab = {}
+        w_raw = {}
 
         def load_g(g, j0, j1):
             tile = keep.tile([P, (j1 - j0) * J], BF16, name="g%d_%d" % (g, j0))
             nc.sync.dma_start(out=tile[:], in_=g_hbm[g][:, j0 * J : j1 * J])
             for j in range(j0, j1):
-                g_sb[4 * g + j] = tile[:, (j - j0) * J : (j - j0 + 1) * J]
+                g_slab[4 * g + j] = tile[:, (j - j0) * J : (j - j0 + 1) * J]
 
         def load_w(a):
-            tile = work.tile([P, 2 * J], BF16, name="w%d" % a, tag="slot", bufs=SLOTS)
-            nc.sync.dma_start(out=tile[:], in_=w_hbm[a])
-            w_sb[a] = tile
+            w_raw[a] = work.tile([P, 2 * J], BF16, name="w_raw", tag="rows", bufs=ROW_BUFFERS)
+            nc.sync.dma_start(out=w_raw[a][:], in_=w_hbm[a])
 
         load_g(0, 0, 1)
         load_w(0)
@@ -65,11 +65,12 @@ def tile_mla_pb_v_kernel(tc, x, freqs_cos, freqs_sin, w_q, grad_out, out_0, out_
         load_w(1)
         load_w(2)
         load_g(0, 2, 4)
-        for a in range(3, 8):
+        for a in range(3, W_TILES):
             load_w(a)
         load_g(1, 0, 4)
+        x_raw = keep.tile([P, 2 * 4 * D], BF16, name="x_raw")
         for g in range(2):
-            nc.sync.dma_start(out=x_sb[:, g * 4 * D : (g + 1) * 4 * D], in_=x_hbm[g])
+            nc.sync.dma_start(out=x_raw[:, g * 4 * D : (g + 1) * 4 * D], in_=x_hbm[g])
 
         ident = keep.tile([P, P], F32, name="ident")
         make_identity(nc, ident[:])
@@ -77,287 +78,266 @@ def tile_mla_pb_v_kernel(tc, x, freqs_cos, freqs_sin, w_q, grad_out, out_0, out_
         sign = keep.tile([P, 2], F32, name="sign")
         nc.vector.memset(sign[:, 0:1], 1.0)
         nc.vector.memset(sign[:, 1:2], -1.0)
-        tab = keep.tile([P, 1024], BF16, name="tab")
-        shape = [P, 2, 128, 2]
-        cos_in = trig[:, 0, :].rearrange("p (a u) -> p u a", u=2).unsqueeze(3).broadcast_to(shape)
-        sin_in = trig[:, 1, :].rearrange("p (a u) -> p u a", u=2).unsqueeze(3).broadcast_to(shape)
-        nc.scalar.copy(out=tab[:, 0:512].rearrange("p (u a e) -> p u a e", u=2, e=2), in_=cos_in)
+        table = keep.tile([P, 2 * BANK], BF16, name="table")
+        both_members = [P, 2, 128, 2]
+        cos_in = trig[:, 0, :].rearrange("p (a u) -> p u a", u=2).unsqueeze(3).broadcast_to(both_members)
+        sin_in = trig[:, 1, :].rearrange("p (a u) -> p u a", u=2).unsqueeze(3).broadcast_to(both_members)
+        nc.scalar.copy(out=table[:, 0:BANK].rearrange("p (u a e) -> p u a e", u=2, e=2), in_=cos_in)
         nc.vector.tensor_tensor(
-            out=tab[:, 512:1024].rearrange("p (u a e) -> p u a e", u=2, e=2),
+            out=table[:, BANK : 2 * BANK].rearrange("p (u a e) -> p u a e", u=2, e=2),
             in0=sin_in,
-            in1=sign[:].unsqueeze(1).unsqueeze(1).broadcast_to(shape),
+            in1=sign[:].unsqueeze(1).unsqueeze(1).broadcast_to(both_members),
             op=MULT,
         )
+        table_turned = keep.tile([P, BANK], F32, name="table_turned")
+        table_psum = psum_table.tile([P, BANK], F32, name="table_psum")
+
+        def transpose_words(bank, blocks):
+            for k, block in enumerate(blocks):
+                nc.tensor.transpose(bank[:, k * P : (k + 1) * P], block, ident[:])
+
+        def quarters(words):
+            return [words[:, k * P : (k + 1) * P] for k in range(4)]
 
         def new_bank():
-            bank = psum.tile([P, 512], F32, name="bank")
+            bank = psum.tile([P, BANK], F32, name="bank")
             return bank
 
-        tab_ps = psum_tab.tile([P, 512], F32, name="tab_ps")
-        tab_t = keep.tile([P, 512], F32, name="tab_t")
-
-        def table_there():
+        def table_first_turn():
             bank = new_bank()
-            words = tab[:].bitcast(F32)
-            for k in range(4):
-                nc.tensor.transpose(bank[:, k * P : (k + 1) * P], words[:, k * P : (k + 1) * P], ident[:])
-            nc.scalar.copy(out=tab_t[:], in_=bank[:])
+            transpose_words(bank, quarters(table[:].bitcast(F32)))
+            nc.scalar.copy(out=table_turned[:], in_=bank[:])
 
-        def table_back():
-            for k in range(4):
-                nc.tensor.transpose(tab_ps[:, k * P : (k + 1) * P], tab_t[:, k * P : (k + 1) * P], ident[:])
+        def table_second_turn():
+            transpose_words(table_psum, quarters(table_turned[:]))
 
-        def codes(name, width):
-            c = keep.tile([P, width], U32, name=name + "c", align_bytes=64)
-            s = keep.tile([P, width], U8, name=name + "s", align_bytes=64)
-            return c, s
+        def mx_pair(pool, name, width, bufs=None):
+            codes = pool.tile([P, width], U32, name=name + "_codes", bufs=bufs, align_bytes=64)
+            scales = pool.tile([P, width], U8, name=name + "_scales", bufs=bufs, align_bytes=64)
+            return codes, scales
 
-        w_mx = {c: codes("w%d" % c, 1024) for c in range(4)}
-        dqt_mx = {s: codes("dqt%d" % s, 256) for s in range(8)}
-        dqk_mx = {q: codes("dqk%d" % q, 1024) for q in range(2)}
-        dq = keep.tile([P, 8 * J], BF16, name="dq", align_bytes=64)
+        def quantize(pair, src, fmt):
+            nc.vector.quantize_mx(out=pair[0][:].bitcast(fmt), scales=pair[1][:], in_=src)
+
+        w_mx = [mx_pair(keep, "w%d" % c, 2 * BANK) for c in range(W_TILES // 2)]
+        dq_feat_mx = [mx_pair(keep, "dq_feat%d" % s, 2 * P) for s in range(SLABS)]
+        dq_tok_mx = [mx_pair(keep, "dq_tok%d" % q, 2 * BANK) for q in range(2)]
+        x_mx = {}
+
+        dq = keep.tile([P, SLABS * J], BF16, name="dq", align_bytes=64)
+        products = {}
 
         def dq_slab(s):
             lo = (2 * (s % 4) + s // 4) * J
             return dq[:, lo : lo + J]
 
-        prod = {}
-        w_t = {}
-        dq_t = {}
-        dq_k = {}
-        x_k = {}
-        x_mx = {}
-        stage = {}
-
-        def table(s, k, h0, h1):
-            src = tab[:] if (s == 0 or not USE_G) else tab_ps[:].bitcast(BF16)
-            rows = src[:, 512 * k : 512 * (k + 1)].rearrange("p (u j w e) -> p u j w e", u=2, j=4, e=2)
-            return rows[:, :, s % 4, :, :].unsqueeze(2).broadcast_to([P, 2, h1 - h0, 32, 2])
-
-        def mul(s, k, h0=0, h1=8):
-            if (s, k) not in prod:
-                prod[s, k] = work.tile([P, J], F32, name="prod%d" % k)
-            gv = g_sb[s].rearrange("p (h w u e) -> p u h w e", h=8, u=2, e=2)[:, :, h0:h1]
+        def multiply(s, k, h0, h1):
+            if (s, k) not in products:
+                products[s, k] = work.tile([P, J], F32, name="product%d" % k)
+            grad = g_slab[s].rearrange("p (h w u e) -> p u h w e", h=HEADS, u=2, e=2)[:, :, h0:h1]
             if k == 1:
-                gv = gv[:, :, :, :, ::-1]
-            out = prod[s, k][:].rearrange("p (u h w e) -> p u h w e", u=2, h=8, e=2)[:, :, h0:h1]
-            nc.vector.tensor_tensor(out=out, in0=gv, in1=table(s, k, h0, h1), op=MULT)
+                grad = grad[:, :, :, :, ::-1]
+            source = table[:] if s == 0 else table_psum[:].bitcast(BF16)
+            rows = source[:, BANK * k : BANK * (k + 1)].rearrange("p (u j w e) -> p u j w e", u=2, j=4, e=2)
+            factor = rows[:, :, s % 4].unsqueeze(2).broadcast_to([P, 2, h1 - h0, 32, 2])
+            out = products[s, k][:].rearrange("p (u h w e) -> p u h w e", u=2, h=HEADS, e=2)[:, :, h0:h1]
+            nc.vector.tensor_tensor(out=out, in0=grad, in1=factor, op=MULT)
 
-        def add(s, eng, lo, hi):
-            out = dq_slab(s)[:, lo:hi]
-            eng.tensor_tensor(out=out, in0=prod[s, 0][:, lo:hi], in1=prod[s, 1][:, lo:hi], op=ADD)
+        def add(engine, s, lo, hi):
+            engine.tensor_tensor(
+                out=dq_slab(s)[:, lo:hi], in0=products[s, 0][:, lo:hi], in1=products[s, 1][:, lo:hi], op=ADD
+            )
 
-        def quantize(pair, src, fmt):
-            nc.vector.quantize_mx(out=pair[0][:].bitcast(fmt), scales=pair[1][:], in_=src)
+        def rotate_begin(s):
+            multiply(s, 0, 0, HEADS)
+            multiply(s, 1, 0, HEADS - 1)
 
-        def turn_w(a, q):
+        def rotate_end(s):
+            multiply(s, 1, HEADS - 1, HEADS)
+            add(nc.vector, s, 0, VECTOR_SUMS)
+            add(nc.gpsimd, s, VECTOR_SUMS, J)
+
+        w_turned = {}
+        dq_turned = {}
+
+        def turn_w(a):
             c = a // 2
-            if c not in w_t:
-                w_t[c] = work.tile([P, 2048], F32, name="w_t", tag="wide", align_bytes=64)
-            bank = new_bank()
-            words = w_sb[a][:].bitcast(F32)
-            for t in range(2):
-                for u in range(2):
-                    lo = t * 512 + q * 256
-                    k = 2 * t + u
-                    nc.tensor.transpose(bank[:, k * P : (k + 1) * P], words[:, lo + u : lo + 256 : 2], ident[:])
-            lo = 1024 * q + 512 * (a % 2)
-            out = w_t[c][:, lo : lo + 512].rearrange("p (r k) -> p r k", k=4)
-            nc.scalar.copy(out=out, in_=bank[:].rearrange("p (k r) -> p r k", k=4))
+            if c not in w_turned:
+                w_turned[c] = work.tile([P, 4 * BANK], F32, name="w_turned", tag="wide", align_bytes=64)
+            words = w_raw[a][:].bitcast(F32).rearrange("p (t q w u) -> p q t u w", t=2, q=2, u=2)
+            for q in range(2):
+                bank = new_bank()
+                transpose_words(bank, [words[:, q, t, u] for t in range(2) for u in range(2)])
+                lo = 2 * BANK * q + BANK * (a % 2)
+                nc.scalar.copy(
+                    out=w_turned[c][:, lo : lo + BANK].rearrange("p (r k) -> p r k", k=4),
+                    in_=bank[:].rearrange("p (k r) -> p r k", k=4),
+                )
 
-        def turn_w_chunk(c):
-            for a in (2 * c, 2 * c + 1):
-                for q in range(2):
-                    turn_w(a, q)
-
-        def quant_w(c):
-            quantize(w_mx[c], w_t[c][:].bitcast(BF16), E4)
+        def quantize_w(c):
+            quantize(w_mx[c], w_turned[c][:].bitcast(BF16), E4M3)
 
         def turn_dq(s):
+            words = dq_slab(s).bitcast(F32).rearrange("p (u q w) -> p q u w", u=2, q=2)
             bank = new_bank()
-            words = dq_slab(s).bitcast(F32)
-            for q in range(2):
-                for u in range(2):
-                    lo = u * 256 + q * P
-                    k = 2 * q + u
-                    nc.tensor.transpose(bank[:, k * P : (k + 1) * P], words[:, lo : lo + P], ident[:])
-            dq_t[s] = work.tile([P, 512], F32, name="dq_t", align_bytes=64)
+            transpose_words(bank, [words[:, q, u] for q in range(2) for u in range(2)])
+            dq_turned[s] = work.tile([P, BANK], F32, name="dq_turned", align_bytes=64)
             nc.scalar.copy(
-                out=dq_t[s][:].rearrange("p (q r u) -> p q r u", q=2, u=2),
+                out=dq_turned[s][:].rearrange("p (q r u) -> p q r u", q=2, u=2),
                 in_=bank[:].rearrange("p (q u r) -> p q r u", q=2, u=2),
             )
 
-        def quant_dq(s):
-            quantize(dqt_mx[s], dq_t[s][:].bitcast(BF16), E5)
+        def quantize_dq_feat(s):
+            quantize(dq_feat_mx[s], dq_turned[s][:].bitcast(BF16), E5M2)
 
-        def weave_dq(q):
-            dq_k[q] = work.tile([P, 4096], BF16, name="dq_k", tag="wide", align_bytes=64)
+        dq_woven = {}
+        x_woven = {}
+
+        def interleave_dq(q):
+            dq_woven[q] = work.tile([P, 8 * BANK], BF16, name="dq_woven", tag="wide", align_bytes=64)
             src = dq[:].rearrange("p (j n q c i) -> p q n c j i", j=4, n=4, q=2, i=4)[:, q]
-            nc.vector.tensor_copy(out=dq_k[q][:].rearrange("p (n c i j) -> p n c j i", n=4, i=4, j=4), in_=src)
+            dst = dq_woven[q][:].rearrange("p (n c i j) -> p n c j i", n=4, i=4, j=4)
+            nc.vector.tensor_copy(out=dst, in_=src)
 
-        def quant_dqk(q):
-            quantize(dqk_mx[q], dq_k[q][:], E5)
+        def quantize_dq_tok(q):
+            quantize(dq_tok_mx[q], dq_woven[q][:], E5M2)
 
-        def weave_x(k, on_scalar=False):
-            x_k[k] = work.tile([P, 2048], BF16, name="x_k", bufs=3, align_bytes=64)
-            src = x_sb[:].rearrange("p (g j k c i) -> p k g c j i", g=2, j=4, k=8, i=4)[:, k]
-            dst = x_k[k][:].rearrange("p (g c i j) -> p g c j i", g=2, i=4, j=4)
-            if on_scalar:
-                nc.scalar.copy(out=dst, in_=src)
-            else:
-                nc.vector.tensor_copy(out=dst, in_=src)
+        def interleave_x(copy, k, g0=0, g1=2):
+            if k not in x_woven:
+                x_woven[k] = work.tile([P, 4 * BANK], BF16, name="x_woven", bufs=3, align_bytes=64)
+            src = x_raw[:].rearrange("p (g j k c i) -> p k g c j i", g=2, j=4, k=X_PIECES, i=4)[:, k, g0:g1]
+            dst = x_woven[k][:].rearrange("p (g c i j) -> p g c j i", g=2, i=4, j=4)[:, g0:g1]
+            copy(out=dst, in_=src)
 
-        def quant_x(k):
-            xc = work.tile([P, 512], U32, name="xc", bufs=7, align_bytes=64)
-            xs = work.tile([P, 512], U8, name="xs", bufs=7, align_bytes=64)
-            x_mx[k] = (xc, xs)
-            quantize(x_mx[k], x_k[k][:], E4)
+        def quantize_x(k):
+            x_mx[k] = mx_pair(work, "x", BANK, bufs=X_PIECES - 1)
+            quantize(x_mx[k], x_woven[k][:], E4M3)
 
-        def product(lhs, lhs_lo, lhs_step, lhs_fmt, rhs, rhs_fmt):
+        rows_out = {}
+
+        def product(lhs, lhs_first, lhs_pass_step, lhs_fmt, rhs, rhs_fmt):
             bank = new_bank()
-            for k in range(2):
-                m_cols = slice(lhs_lo + k * lhs_step, lhs_lo + k * lhs_step + P)
-                n_cols = slice(512 * k, 512 * (k + 1))
+            for n in range(2):
+                m_cols = slice(lhs_first + n * lhs_pass_step, lhs_first + n * lhs_pass_step + P)
+                n_cols = slice(BANK * n, BANK * (n + 1))
                 nc.tensor.matmul_mx(
                     out=bank[:],
                     lhsT=lhs[0][:, m_cols].bitcast(lhs_fmt),
                     lhsT_scale=lhs[1][:, m_cols],
                     rhs=rhs[0][:, n_cols].bitcast(rhs_fmt),
                     rhs_scale=rhs[1][:, n_cols],
-                    start=(k == 0),
-                    stop=(k == 1),
+                    start=(n == 0),
+                    stop=(n == 1),
                 )
             return bank
 
-        def evac(out, in_, on_vector):
-            if on_vector:
-                nc.vector.tensor_copy(out=out, in_=in_)
-            else:
-                nc.scalar.copy(out=out, in_=in_)
+        def out_rows(key):
+            if key not in rows_out:
+                rows_out[key] = work.tile([P, 2 * BANK], F32, name="rows_out", tag="rows", bufs=ROW_BUFFERS)
+            return rows_out[key]
 
-        def dx_bank(s, c, on_vector=False):
-            bank = product(dqt_mx[s], 0, P, E5, w_mx[c], E4)
-            key = ("dx", s, c // 2)
-            if key not in stage:
-                stage[key] = work.tile([P, 1024], F32, name="stage", tag="slot", bufs=SLOTS)
-            evac(stage[key][:, 512 * (c % 2) : 512 * (c % 2 + 1)], bank[:], on_vector)
+        def dx_bank(s, c):
+            bank = product(dq_feat_mx[s], 0, P, E5M2, w_mx[c], E4M3)
+            rows = out_rows(("dx", s, c // 2))
+            nc.scalar.copy(out=rows[:, BANK * (c % 2) : BANK * (c % 2 + 1)], in_=bank[:])
             if c % 2 == 1:
-                h = c // 2
-                nc.sync.dma_start(out=dx_hbm[s // 4][s % 4][:, 1024 * h : 1024 * (h + 1)], in_=stage[key][:])
+                nc.sync.dma_start(out=dx_hbm[s // 4][s % 4][:, BANK * (c - 1) : BANK * (c + 1)], in_=rows[:])
 
-        def dw_bank(m, q, on_vector=False, split=False):
-            bank = product(x_mx[m // 2], (m % 2) * P, 256, E4, dqk_mx[q], E5)
-            key = ("dw", m)
-            if key not in stage:
-                stage[key] = work.tile([P, 1024], F32, name="stage", tag="slot", bufs=SLOTS)
-            half = stage[key][:, 512 * q : 512 * (q + 1)]
-            evac(half.rearrange("p (w u e) -> p w u e", u=2, e=2), bank[:].rearrange("p (u w e) -> p w u e", u=2, e=2), on_vector)
-            if split:
-                nc.sync.dma_start(out=out_1[m * P : (m + 1) * P, 512 * q : 512 * (q + 1)], in_=half)
+        def dw_bank(m, q):
+            bank = product(x_mx[m // 2], (m % 2) * P, 2 * P, E4M3, dq_tok_mx[q], E5M2)
+            rows = out_rows(("dw", m))
+            half = rows[:, BANK * q : BANK * (q + 1)]
+            copy = nc.vector.tensor_copy if m // 2 >= SHARED_FROM and q == 1 else nc.scalar.copy
+            copy(
+                out=half.rearrange("p (w u e) -> p w u e", u=2, e=2),
+                in_=bank[:].rearrange("p (u w e) -> p w u e", u=2, e=2),
+            )
+            hbm_rows = out_1[m * P : (m + 1) * P, :]
+            if m == 2 * X_PIECES - 1:
+                nc.sync.dma_start(out=hbm_rows[:, BANK * q : BANK * (q + 1)], in_=half)
             elif q == 1:
-                nc.sync.dma_start(out=out_1[m * P : (m + 1) * P, :], in_=stage[key][:])
+                nc.sync.dma_start(out=hbm_rows, in_=rows[:])
 
-        def rotate_head(s):
-            mul(s, 0)
-            if USE_G and s < 7:
-                mul(s, 1, 0, 8 - TAIL_HEADS)
-            else:
-                mul(s, 1)
+        table_first_turn()
+        turn_w(0)
+        table_second_turn()
+        turn_w(1)
+        rotate_begin(0)
+        rotate_end(0)
 
-        def rotate_tail(s):
-            if USE_G and s < 7:
-                if V_COLS:
-                    add(s, nc.vector, 0, V_COLS)
-                mul(s, 1, 8 - TAIL_HEADS, 8)
-                add(s, nc.gpsimd, V_COLS, J)
-            else:
-                add(s, nc.vector, 0, J)
-
-        table_there()
-        turn_w(0, 0)
-        turn_w(0, 1)
-        table_back()
-        turn_w(1, 0)
-        turn_w(1, 1)
-        rotate_head(0)
-        rotate_tail(0)
-        rotate_head(1)
-        quant_w(0)
-        rotate_tail(1)
-        turn_w(2, 0)
-        turn_w(2, 1)
+        rotate_begin(1)
+        quantize_w(0)
+        rotate_end(1)
+        turn_w(2)
         turn_dq(0)
-        turn_w(3, 0)
-        turn_w(3, 1)
-        rotate_head(2)
-        quant_dq(0)
-        quant_w(1)
-        rotate_tail(2)
-        turn_w(4, 0)
-        turn_w(4, 1)
+        turn_w(3)
+
+        rotate_begin(2)
+        quantize_dq_feat(0)
+        quantize_w(1)
+        rotate_end(2)
+        turn_w(4)
+        turn_w(5)
         turn_dq(1)
-        turn_w(5, 0)
-        turn_w(5, 1)
         dx_bank(0, 0)
-        turn_w(6, 0)
-        turn_w(6, 1)
+        turn_w(6)
         dx_bank(0, 1)
-        rotate_head(3)
-        quant_dq(1)
-        quant_w(2)
-        rotate_tail(3)
-        turn_w(7, 0)
-        turn_w(7, 1)
+        turn_w(7)
+
+        rotate_begin(3)
+        quantize_dq_feat(1)
+        quantize_w(2)
+        rotate_end(3)
         turn_dq(2)
-        dx_bank(1, 0)
-        dx_bank(1, 1)
-        dx_bank(0, 2)
-        dx_bank(1, 2)
-        rotate_head(4)
-        quant_w(3)
-        quant_dq(2)
-        rotate_tail(4)
+        for s, c in ((1, 0), (1, 1), (0, 2), (1, 2)):
+            dx_bank(s, c)
+
+        rotate_begin(4)
+        quantize_w(3)
+        quantize_dq_feat(2)
+        rotate_end(4)
         turn_dq(3)
-        dx_bank(0, 3)
-        dx_bank(1, 3)
-        for s in range(5, 8):
-            rotate_head(s)
-            quant_dq(s - 2)
-            rotate_tail(s)
-            for c in range(2):
-                dx_bank(s - 3, c)
+        for s in range(2):
+            dx_bank(s, 3)
+
+        for s in range(5, SLABS):
+            if s < SLABS - 1:
+                rotate_begin(s)
+                quantize_dq_feat(s - 2)
+                rotate_end(s)
+            else:
+                multiply(s, 0, 0, HEADS)
+                multiply(s, 1, 0, HEADS)
+                quantize_dq_feat(s - 2)
+                add(nc.vector, s, 0, J)
+            dx_bank(s - 3, 0)
+            dx_bank(s - 3, 1)
             turn_dq(s - 1)
-            for c in range(2, 4):
-                dx_bank(s - 3, c)
-        quant_dq(6)
-        turn_dq(7)
-        weave_x(0, on_scalar=True)
-        for c in range(2):
-            dx_bank(5, c)
-        for c in range(2, 4):
-            dx_bank(5, c)
-        weave_dq(0)
-        quant_dq(7)
-        quant_dqk(0)
-        quant_x(0)
-        weave_dq(1)
-        for c in range(4):
-            dx_bank(6, c)
-        weave_x(1)
-        quant_dqk(1)
-        for c in range(4):
-            dx_bank(7, c)
+            dx_bank(s - 3, 2)
+            dx_bank(s - 3, 3)
+
+        turn_dq(SLABS - 1)
+        interleave_x(nc.scalar.copy, 0, 0, 1)
+        interleave_x(nc.vector.tensor_copy, 0, 1, 2)
+        interleave_dq(0)
+        quantize_dq_feat(SLABS - 2)
+        quantize_dq_feat(SLABS - 1)
+        quantize_dq_tok(0)
+        quantize_x(0)
+        interleave_dq(1)
+        interleave_x(nc.vector.tensor_copy, 1)
+        quantize_dq_tok(1)
+        for s in range(SLABS - 3, SLABS):
+            for c in range(4):
+                dx_bank(s, c)
         for q in range(2):
             for m in range(2):
-                dw_bank(m, q, split=True)
-        for k in range(1, 8):
-            if k < 7:
-                weave_x(k + 1)
-            quant_x(k)
-            if k == 6:
-                for m in (2, 3):
-                    for q in range(2):
-                        dw_bank(m, q)
-        for m in range(4, 16):
+                dw_bank(m, q)
+
+        for k in range(1, X_PIECES):
+            if k + 1 < X_PIECES:
+                interleave_x(nc.vector.tensor_copy, k + 1)
+            quantize_x(k)
+        for m in range(2, 2 * X_PIECES):
             for q in range(2):
-                dw_bank(m, q, on_vector=(m >= 2 * V_FROM and q == 1), split=(m == 15))
+                dw_bank(m, q)

from contextlib import ExitStack

import concourse.mybir as mybir
from concourse.masks import make_identity

F32 = mybir.dt.float32
BF16 = mybir.dt.bfloat16
U32 = mybir.dt.uint32
U8 = mybir.dt.uint8
E4M3 = mybir.dt.float8_e4m3fn_x4
E5M2 = mybir.dt.float8_e5m2_x4
MULT = mybir.AluOpType.mult
ADD = mybir.AluOpType.add

T, D, J = 1024, 2048, 1024
FLOPS = 2 * 2 * T * D * J
P = 128
BANK = 512
HEADS = 8
SLABS = 8
W_TILES = 8
X_PIECES = 8

VECTOR_SUMS = 256
SHARED_FROM = 5
ROW_BUFFERS = W_TILES + 5


def tile_mla_pb_v_kernel(tc, x, freqs_cos, freqs_sin, w_q, grad_out, out_0, out_1):
    nc = tc.nc
    g_hbm = grad_out.rearrange("b s h d -> (b s) (h d)").rearrange("(g p j) f -> g p (j f)", g=2, j=4)
    x_hbm = x.rearrange("b s d -> (b s) d").rearrange("(g p j) d -> g p (j d)", g=2, j=4)
    dx_hbm = out_0.rearrange("b s d -> (b s) d").rearrange("(g p j) d -> g j p d", g=2, j=4)
    w_hbm = w_q.rearrange("(a p t) f -> a p (t f)", p=P, t=2)

    with ExitStack() as ctx:
        keep = ctx.enter_context(tc.tile_pool(name="keep", bufs=1))
        work = ctx.enter_context(tc.tile_pool(name="work", bufs=2))
        psum = ctx.enter_context(tc.psum_pool(name="psum", bufs=7))
        psum_table = ctx.enter_context(tc.psum_pool(name="psum_table", bufs=1))
        ctx.enter_context(tc.manual_schedule())

        trig = keep.tile([P, 2, 256], BF16, name="trig")
        for k, src in enumerate((freqs_cos, freqs_sin)):
            for half in range(2):
                rows = src.rearrange("(p j) i -> p (j i)", j=4)
                nc.sync.dma_start(out=trig[64 * half : 64 * half + 64, k, :], in_=rows)

        g_slab = {}
        w_raw = {}

        def load_g(g, j0, j1):
            tile = keep.tile([P, (j1 - j0) * J], BF16, name="g%d_%d" % (g, j0))
            nc.sync.dma_start(out=tile[:], in_=g_hbm[g][:, j0 * J : j1 * J])
            for j in range(j0, j1):
                g_slab[4 * g + j] = tile[:, (j - j0) * J : (j - j0 + 1) * J]

        def load_w(a):
            w_raw[a] = work.tile([P, 2 * J], BF16, name="w_raw", tag="rows", bufs=ROW_BUFFERS)
            nc.sync.dma_start(out=w_raw[a][:], in_=w_hbm[a])

        load_g(0, 0, 1)
        load_w(0)
        load_g(0, 1, 2)
        load_w(1)
        load_w(2)
        load_g(0, 2, 4)
        for a in range(3, W_TILES):
            load_w(a)
        load_g(1, 0, 4)
        x_raw = keep.tile([P, 2 * 4 * D], BF16, name="x_raw")
        for g in range(2):
            nc.sync.dma_start(out=x_raw[:, g * 4 * D : (g + 1) * 4 * D], in_=x_hbm[g])

        ident = keep.tile([P, P], F32, name="ident")
        make_identity(nc, ident[:])

        sign = keep.tile([P, 2], F32, name="sign")
        nc.vector.memset(sign[:, 0:1], 1.0)
        nc.vector.memset(sign[:, 1:2], -1.0)
        table = keep.tile([P, 2 * BANK], BF16, name="table")
        both_members = [P, 2, 128, 2]
        cos_in = trig[:, 0, :].rearrange("p (a u) -> p u a", u=2).unsqueeze(3).broadcast_to(both_members)
        sin_in = trig[:, 1, :].rearrange("p (a u) -> p u a", u=2).unsqueeze(3).broadcast_to(both_members)
        nc.scalar.copy(out=table[:, 0:BANK].rearrange("p (u a e) -> p u a e", u=2, e=2), in_=cos_in)
        nc.vector.tensor_tensor(
            out=table[:, BANK : 2 * BANK].rearrange("p (u a e) -> p u a e", u=2, e=2),
            in0=sin_in,
            in1=sign[:].unsqueeze(1).unsqueeze(1).broadcast_to(both_members),
            op=MULT,
        )
        table_turned = keep.tile([P, BANK], F32, name="table_turned")
        table_psum = psum_table.tile([P, BANK], F32, name="table_psum")

        def transpose_words(bank, blocks):
            for k, block in enumerate(blocks):
                nc.tensor.transpose(bank[:, k * P : (k + 1) * P], block, ident[:])

        def quarters(words):
            return [words[:, k * P : (k + 1) * P] for k in range(4)]

        def new_bank():
            bank = psum.tile([P, BANK], F32, name="bank")
            return bank

        def table_first_turn():
            bank = new_bank()
            transpose_words(bank, quarters(table[:].bitcast(F32)))
            nc.scalar.copy(out=table_turned[:], in_=bank[:])

        def table_second_turn():
            transpose_words(table_psum, quarters(table_turned[:]))

        def mx_pair(pool, name, width, bufs=None):
            codes = pool.tile([P, width], U32, name=name + "_codes", bufs=bufs, align_bytes=64)
            scales = pool.tile([P, width], U8, name=name + "_scales", bufs=bufs, align_bytes=64)
            return codes, scales

        def quantize(pair, src, fmt):
            nc.vector.quantize_mx(out=pair[0][:].bitcast(fmt), scales=pair[1][:], in_=src)

        w_mx = [mx_pair(keep, "w%d" % c, 2 * BANK) for c in range(W_TILES // 2)]
        dq_feat_mx = [mx_pair(keep, "dq_feat%d" % s, 2 * P) for s in range(SLABS)]
        dq_tok_mx = [mx_pair(keep, "dq_tok%d" % q, 2 * BANK) for q in range(2)]
        x_mx = {}

        dq = keep.tile([P, SLABS * J], BF16, name="dq", align_bytes=64)
        products = {}

        def dq_slab(s):
            lo = (2 * (s % 4) + s // 4) * J
            return dq[:, lo : lo + J]

        def multiply(s, k, h0, h1):
            if (s, k) not in products:
                products[s, k] = work.tile([P, J], F32, name="product%d" % k)
            grad = g_slab[s].rearrange("p (h w u e) -> p u h w e", h=HEADS, u=2, e=2)[:, :, h0:h1]
            if k == 1:
                grad = grad[:, :, :, :, ::-1]
            source = table[:] if s == 0 else table_psum[:].bitcast(BF16)
            rows = source[:, BANK * k : BANK * (k + 1)].rearrange("p (u j w e) -> p u j w e", u=2, j=4, e=2)
            factor = rows[:, :, s % 4].unsqueeze(2).broadcast_to([P, 2, h1 - h0, 32, 2])
            out = products[s, k][:].rearrange("p (u h w e) -> p u h w e", u=2, h=HEADS, e=2)[:, :, h0:h1]
            nc.vector.tensor_tensor(out=out, in0=grad, in1=factor, op=MULT)

        def add(engine, s, lo, hi):
            engine.tensor_tensor(
                out=dq_slab(s)[:, lo:hi], in0=products[s, 0][:, lo:hi], in1=products[s, 1][:, lo:hi], op=ADD
            )

        def rotate_begin(s):
            multiply(s, 0, 0, HEADS)
            multiply(s, 1, 0, HEADS - 1)

        def rotate_end(s):
            multiply(s, 1, HEADS - 1, HEADS)
            add(nc.vector, s, 0, VECTOR_SUMS)
            add(nc.gpsimd, s, VECTOR_SUMS, J)

        w_turned = {}
        dq_turned = {}

        def turn_w(a):
            c = a // 2
            if c not in w_turned:
                w_turned[c] = work.tile([P, 4 * BANK], F32, name="w_turned", tag="wide", align_bytes=64)
            words = w_raw[a][:].bitcast(F32).rearrange("p (t q w u) -> p q t u w", t=2, q=2, u=2)
            for q in range(2):
                bank = new_bank()
                transpose_words(bank, [words[:, q, t, u] for t in range(2) for u in range(2)])
                lo = 2 * BANK * q + BANK * (a % 2)
                nc.scalar.copy(
                    out=w_turned[c][:, lo : lo + BANK].rearrange("p (r k) -> p r k", k=4),
                    in_=bank[:].rearrange("p (k r) -> p r k", k=4),
                )

        def quantize_w(c):
            quantize(w_mx[c], w_turned[c][:].bitcast(BF16), E4M3)

        def turn_dq(s):
            words = dq_slab(s).bitcast(F32).rearrange("p (u q w) -> p q u w", u=2, q=2)
            bank = new_bank()
            transpose_words(bank, [words[:, q, u] for q in range(2) for u in range(2)])
            dq_turned[s] = work.tile([P, BANK], F32, name="dq_turned", align_bytes=64)
            nc.scalar.copy(
                out=dq_turned[s][:].rearrange("p (q r u) -> p q r u", q=2, u=2),
                in_=bank[:].rearrange("p (q u r) -> p q r u", q=2, u=2),
            )

        def quantize_dq_feat(s):
            quantize(dq_feat_mx[s], dq_turned[s][:].bitcast(BF16), E5M2)

        dq_woven = {}
        x_woven = {}

        def interleave_dq(q):
            dq_woven[q] = work.tile([P, 8 * BANK], BF16, name="dq_woven", tag="wide", align_bytes=64)
            src = dq[:].rearrange("p (j n q c i) -> p q n c j i", j=4, n=4, q=2, i=4)[:, q]
            dst = dq_woven[q][:].rearrange("p (n c i j) -> p n c j i", n=4, i=4, j=4)
            nc.vector.tensor_copy(out=dst, in_=src)

        def quantize_dq_tok(q):
            quantize(dq_tok_mx[q], dq_woven[q][:], E5M2)

        def interleave_x(copy, k, g0=0, g1=2):
            if k not in x_woven:
                x_woven[k] = work.tile([P, 4 * BANK], BF16, name="x_woven", bufs=3, align_bytes=64)
            src = x_raw[:].rearrange("p (g j k c i) -> p k g c j i", g=2, j=4, k=X_PIECES, i=4)[:, k, g0:g1]
            dst = x_woven[k][:].rearrange("p (g c i j) -> p g c j i", g=2, i=4, j=4)[:, g0:g1]
            copy(out=dst, in_=src)

        def quantize_x(k):
            x_mx[k] = mx_pair(work, "x", BANK, bufs=X_PIECES - 1)
            quantize(x_mx[k], x_woven[k][:], E4M3)

        rows_out = {}

        def product(lhs, lhs_first, lhs_pass_step, lhs_fmt, rhs, rhs_fmt):
            bank = new_bank()
            for n in range(2):
                m_cols = slice(lhs_first + n * lhs_pass_step, lhs_first + n * lhs_pass_step + P)
                n_cols = slice(BANK * n, BANK * (n + 1))
                nc.tensor.matmul_mx(
                    out=bank[:],
                    lhsT=lhs[0][:, m_cols].bitcast(lhs_fmt),
                    lhsT_scale=lhs[1][:, m_cols],
                    rhs=rhs[0][:, n_cols].bitcast(rhs_fmt),
                    rhs_scale=rhs[1][:, n_cols],
                    start=(n == 0),
                    stop=(n == 1),
                )
            return bank

        def out_rows(key):
            if key not in rows_out:
                rows_out[key] = work.tile([P, 2 * BANK], F32, name="rows_out", tag="rows", bufs=ROW_BUFFERS)
            return rows_out[key]

        def dx_bank(s, c):
            bank = product(dq_feat_mx[s], 0, P, E5M2, w_mx[c], E4M3)
            rows = out_rows(("dx", s, c // 2))
            nc.scalar.copy(out=rows[:, BANK * (c % 2) : BANK * (c % 2 + 1)], in_=bank[:])
            if c % 2 == 1:
                nc.sync.dma_start(out=dx_hbm[s // 4][s % 4][:, BANK * (c - 1) : BANK * (c + 1)], in_=rows[:])

        def dw_bank(m, q):
            bank = product(x_mx[m // 2], (m % 2) * P, 2 * P, E4M3, dq_tok_mx[q], E5M2)
            rows = out_rows(("dw", m))
            half = rows[:, BANK * q : BANK * (q + 1)]
            copy = nc.vector.tensor_copy if m // 2 >= SHARED_FROM and q == 1 else nc.scalar.copy
            copy(
                out=half.rearrange("p (w u e) -> p w u e", u=2, e=2),
                in_=bank[:].rearrange("p (u w e) -> p w u e", u=2, e=2),
            )
            hbm_rows = out_1[m * P : (m + 1) * P, :]
            if m == 2 * X_PIECES - 1:
                nc.sync.dma_start(out=hbm_rows[:, BANK * q : BANK * (q + 1)], in_=half)
            elif q == 1:
                nc.sync.dma_start(out=hbm_rows, in_=rows[:])

        table_first_turn()
        turn_w(0)
        table_second_turn()
        turn_w(1)
        rotate_begin(0)
        rotate_end(0)

        rotate_begin(1)
        quantize_w(0)
        rotate_end(1)
        turn_w(2)
        turn_dq(0)
        turn_w(3)

        rotate_begin(2)
        quantize_dq_feat(0)
        quantize_w(1)
        rotate_end(2)
        turn_w(4)
        turn_w(5)
        turn_dq(1)
        dx_bank(0, 0)
        turn_w(6)
        dx_bank(0, 1)
        turn_w(7)

        rotate_begin(3)
        quantize_dq_feat(1)
        quantize_w(2)
        rotate_end(3)
        turn_dq(2)
        for s, c in ((1, 0), (1, 1), (0, 2), (1, 2)):
            dx_bank(s, c)

        rotate_begin(4)
        quantize_w(3)
        quantize_dq_feat(2)
        rotate_end(4)
        turn_dq(3)
        for s in range(2):
            dx_bank(s, 3)

        for s in range(5, SLABS):
            if s < SLABS - 1:
                rotate_begin(s)
                quantize_dq_feat(s - 2)
                rotate_end(s)
            else:
                multiply(s, 0, 0, HEADS)
                multiply(s, 1, 0, HEADS)
                quantize_dq_feat(s - 2)
                add(nc.vector, s, 0, J)
            dx_bank(s - 3, 0)
            dx_bank(s - 3, 1)
            turn_dq(s - 1)
            dx_bank(s - 3, 2)
            dx_bank(s - 3, 3)

        turn_dq(SLABS - 1)
        interleave_x(nc.scalar.copy, 0, 0, 1)
        interleave_x(nc.vector.tensor_copy, 0, 1, 2)
        interleave_dq(0)
        quantize_dq_feat(SLABS - 2)
        quantize_dq_feat(SLABS - 1)
        quantize_dq_tok(0)
        quantize_x(0)
        interleave_dq(1)
        interleave_x(nc.vector.tensor_copy, 1)
        quantize_dq_tok(1)
        for s in range(SLABS - 3, SLABS):
            for c in range(4):
                dx_bank(s, c)
        for q in range(2):
            for m in range(2):
                dw_bank(m, q)

        for k in range(1, X_PIECES):
            if k + 1 < X_PIECES:
                interleave_x(nc.vector.tensor_copy, k + 1)
            quantize_x(k)
        for m in range(2, 2 * X_PIECES):
            for q in range(2):
                dw_bank(m, q)
